import numpy as np
import ml_dtypes


def mxq(x, axis, fmt="e4m3"):
    dtype, down = {"e4m3": (ml_dtypes.float8_e4m3fn, 7), "e5m2": (ml_dtypes.float8_e5m2, 14)}[fmt]
    v = np.moveaxis(np.asarray(x, np.float32).astype(ml_dtypes.bfloat16).astype(np.float64), axis, -1)
    blocks = v.reshape(v.shape[:-1] + (-1, 32))
    amax = np.abs(blocks).max(-1, keepdims=True)
    byte = np.maximum(np.where(amax > 0, np.frexp(amax)[1] - 1 + 127, 0) - down, 1)
    scale = np.exp2(byte - 127.0)
    codes = (blocks / scale).astype(np.float32).astype(dtype).astype(np.float64)
    return np.moveaxis((codes * scale).reshape(v.shape), -1, axis)


WIDE = False


def mx_kscale(k):
    if not WIDE:
        return np.ones(k)
    levels = np.array([10, -10, 5, -5, 0])
    if k % 512:
        return np.exp2(np.random.permutation(np.resize(levels, k // 32))).repeat(32)
    a = np.empty((k // 512, 16))
    for p in range(k // 512):
        a[p, :8] = np.random.permutation(np.resize(levels, 8))
        for g in range(8):
            far = levels[np.abs(levels - a[p, g]) >= 10]
            a[p, g + 8] = far[np.random.randint(len(far))]
    return np.exp2(a.ravel()).repeat(32)


BF16 = ml_dtypes.bfloat16


def bf(x):
    return np.asarray(x, np.float32).astype(BF16)


def f64(x):
    return np.asarray(x).astype(np.float64)


B, N, D, LAYER_NUM = 4, 2048, 512, 2


def setup_inputs():
    fin = mx_kscale(D)
    user = bf(np.random.standard_normal((B, N, D)) * fin)
    parts = []
    for l in range(LAYER_NUM):
        fout = mx_kscale(D) if l + 1 < LAYER_NUM else np.ones(D)
        parts.append((np.random.standard_normal((B, D, D)) * 1.2 / np.sqrt(D) / fin[:, None] * fout).reshape(B, D * D))
        parts.append(np.random.standard_normal((B, D)) * 0.5 * fout)
        fin = fout
    return {"user_emb": user, "item_emb": bf(np.concatenate(parts, axis=1))}


def reference(user_emb, item_emb):
    x = f64(user_emb)
    item = f64(item_emb)
    nb = x.shape[0]
    off = 0
    for _ in range(LAYER_NUM):
        W = item[:, off:off + D * D].reshape(nb, D, D)
        off += D * D
        b = item[:, off:off + D].reshape(nb, 1, D)
        off += D
        x = np.maximum((mxq(x, 2, "e4m3") @ mxq(W, 1, "e4m3")) + b, 0.0)
    return x

@@ -1,0 +1,341 @@
+from contextlib import ExitStack
+
+import concourse.mybir as mybir
+from concourse.masks import make_identity
+
+F32 = mybir.dt.float32
+BF16 = mybir.dt.bfloat16
+U32 = mybir.dt.uint32
+U8 = mybir.dt.uint8
+FP8X4 = mybir.dt.float8_e4m3fn_x4
+ACT = mybir.ActivationFunctionType
+ALU = mybir.AluOpType
+
+PINNED = True
+RELU_A = "S"
+RELU_B = "SV"
+HR = "G"
+HR_PARTS = 4
+
+P = 128
+NB = 4
+NTOK = 2048
+D = 512
+PACK = 4
+TILES = 4
+CHUNK = TILES * P
+NCH = NTOK // CHUNK
+APP = NTOK // P
+TOTAL = NB * NCH
+OFF_W = (0, D * D + D)
+OFF_B0 = D * D
+OFF_B1 = 2 * D * D + D
+FLT_MAX = 3.4028234663852886e38
+
+FLOPS = 2 * NB * NTOK * D * D * 2
+
+
+def tile_can_t_kernel(tc, user_emb, item_emb, out):
+    nc = tc.nc
+    with ExitStack() as ctx:
+        if PINNED:
+            ctx.enter_context(tc.manual_schedule())
+        const = ctx.enter_context(tc.tile_pool(name="const", bufs=1))
+        wstage = ctx.enter_context(tc.tile_pool(name="wstage", bufs=2))
+        xq = ctx.enter_context(tc.tile_pool(name="xq", bufs=2))
+        hstage = ctx.enter_context(tc.tile_pool(name="hstage", bufs=2))
+        hq = ctx.enter_context(tc.tile_pool(name="hq", bufs=2))
+        ostage = ctx.enter_context(tc.tile_pool(name="ostage", bufs=4))
+        ps_t = ctx.enter_context(tc.psum_pool(name="ps_t", bufs=2))
+        ps_h = ctx.enter_context(tc.psum_pool(name="ps_h", bufs=3))
+        ps_o = ctx.enter_context(tc.psum_pool(name="ps_o", bufs=3))
+
+        wraw = {}
+        xraw = {}
+
+        def load_w(b, layer):
+            t = const.tile([P, PACK, D], BF16, name="wraw%d%d" % (b, layer))
+            flat = item_emb[b, OFF_W[layer] : OFF_W[layer] + D * D]
+            nc.sync.dma_start(out=t[:], in_=flat.rearrange("(p j c) -> p j c", p=P, j=PACK, c=D))
+            wraw[(b, layer)] = t
+
+        def load_x(i):
+            b, c = divmod(i, NCH)
+            t = const.tile([P, TILES, D], BF16, name="xraw%d" % i)
+            src = user_emb[b].rearrange("(p a) k -> p a k", a=APP)
+            nc.sync.dma_start(out=t[:], in_=src[:, TILES * c : TILES * (c + 1), :])
+            xraw[i] = t
+
+        b0rows = const.tile([P, D], BF16, name="b0rows")
+        nc.vector.memset(b0rows[:], 0.0)
+        b1row = const.tile([P, NB * D], BF16, name="b1row")
+        nc.vector.memset(b1row[:], 0.0)
+        ones = const.tile([P, P], BF16, name="ones")
+        nc.vector.memset(ones[:], 1.0)
+
+        load_w(0, 0)
+        load_x(0)
+        nc.sync.dma_start(out=b0rows[0:NB, :], in_=item_emb[:, OFF_B0 : OFF_B0 + D])
+        nc.sync.dma_start(
+            out=b1row[0:1, :].rearrange("o (b e) -> o b e", b=NB),
+            in_=item_emb[:, OFF_B1 : OFF_B1 + D].unsqueeze(0),
+        )
+        load_w(0, 1)
+        for i in range(1, 5):
+            load_x(i)
+        load_w(1, 0)
+        load_w(1, 1)
+        for i in range(5, 8):
+            load_x(i)
+
+        ident_f = const.tile([P, P], F32, name="ident_f")
+        make_identity(nc, ident_f[:])
+        ident_b = const.tile([P, P], BF16, name="ident_b")
+        make_identity(nc, ident_b[:])
+
+        wcodes = const.tile([P, 2 * NB, D], U32, name="wcodes", align_bytes=64)
+        wscales = const.tile([P, 2 * NB, D], U8, name="wscales", align_bytes=64)
+        wgrp = {}
+
+        def regroup_w(b, layer, part):
+            if part is None or part == 0:
+                wgrp[(b, layer)] = wstage.tile([P, D, PACK], BF16, name="wgrp", tag="wgrp", align_bytes=64)
+            if layer == 0:
+                dst = wgrp[(b, layer)][:].rearrange("p (t c i) j -> p t c j i", t=PACK, i=4)
+                src = wraw[(b, layer)][:].rearrange("p j (c i t) -> p t c j i", t=PACK, i=4)
+                pieces = [(dst[:, t], src[:, t]) for t in range(PACK)]
+            else:
+                dst = wgrp[(b, layer)][:].rearrange("p (q c i) j -> p q c j i", q=HR_PARTS, i=4)
+                src = wraw[(b, layer)][:].rearrange("p j (q c i) -> p q c j i", q=HR_PARTS, i=4)
+                pieces = [(dst[:, t], src[:, t]) for t in range(PACK)]
+            if part is None:
+                for piece_dst, piece_src in pieces:
+                    nc.vector.tensor_copy(out=piece_dst, in_=piece_src)
+                return
+            piece_dst, piece_src = pieces[part]
+            if HR == "S":
+                nc.scalar.copy(out=piece_dst, in_=piece_src)
+            else:
+                nc.gpsimd.tensor_scalar(
+                    out=piece_dst,
+                    in0=piece_src,
+                    scalar1=1.0,
+                    scalar2=0.0,
+                    op0=ALU.mult,
+                    op1=ALU.add,
+                )
+
+        def quant_w(b, layer):
+            j = 2 * b + layer
+            nc.vector.quantize_mx(
+                out=wcodes[:, j, :].bitcast(FP8X4),
+                scales=wscales[:, j, :],
+                in_=wgrp[(b, layer)][:].rearrange("p c t -> p (c t)"),
+            )
+
+        st = {}
+
+        def transposes(i, half):
+            xt = ps_t.tile([P, 2, 2, P], F32, name="xt", tag="t")
+            for a2 in range(2):
+                words = xraw[i][:, 2 * half + a2, :].bitcast(F32)
+                for u in range(2):
+                    nc.tensor.transpose(xt[:, a2, u, :], words[:, u : 2 * P : 2], ident_f[:])
+            st[("xt", i, half)] = xt
+
+        def copy_x(i, half):
+            if half == 0:
+                st[("xgrp", i)] = xq.tile([P, CHUNK * PACK], BF16, name="xgrp", tag="xgrp", align_bytes=64)
+            xw = st[("xgrp", i)][:].bitcast(F32).rearrange("p (a r u) -> p a r u", a=TILES, r=P, u=2)
+            nc.scalar.copy(
+                out=xw[:, 2 * half : 2 * half + 2, :, :],
+                in_=st[("xt", i, half)][:].rearrange("p a u r -> p a r u"),
+            )
+
+        def quant_x(i):
+            xcodes = xq.tile([P, CHUNK], U32, name="xcodes", tag="xcodes", align_bytes=64)
+            xscales = xq.tile([P, CHUNK], U8, name="xscales", tag="xscales", align_bytes=64)
+            nc.vector.quantize_mx(out=xcodes[:].bitcast(FP8X4), scales=xscales[:], in_=st[("xgrp", i)][:])
+            st[("xc", i)] = (xcodes, xscales)
+
+        def layer1(i, t):
+            b = i // NCH
+            xcodes, xscales = st[("xc", i)]
+            hp = ps_h.tile([P, CHUNK], F32, name="hp", tag="h")
+            nc.tensor.matmul_mx(
+                out=hp[:],
+                lhsT=wcodes[:, 2 * b, P * t : P * (t + 1)].bitcast(FP8X4),
+                lhsT_scale=wscales[:, 2 * b, P * t : P * (t + 1)],
+                rhs=xcodes[:].bitcast(FP8X4),
+                rhs_scale=xscales[:],
+                start=True,
+                stop=True,
+            )
+            st[("hp", i, t)] = hp
+
+        def act(i, t):
+            b = i // NCH
+            if t == 0:
+                st[("hT", i)] = hstage.tile([P, PACK, CHUNK], BF16, name="hT", tag="hT")
+            nc.scalar.activation(
+                out=st[("hT", i)][:, t, :],
+                in_=st[("hp", i, t)][:],
+                func=ACT.Relu,
+                bias=b0_sb[:, t, b : b + 1],
+                scale=1.0,
+            )
+
+        def regroup_h(i):
+            hgrp = hq.tile([P, CHUNK, PACK], BF16, name="hgrp", tag="hgrp", align_bytes=64)
+            nc.vector.tensor_copy(
+                out=hgrp[:].rearrange("p (c i) t -> p c t i", i=4),
+                in_=st[("hT", i)][:].rearrange("p t (c i) -> p c t i", i=4),
+            )
+            st[("hgrp", i)] = hgrp
+
+        def quant_h(i):
+            hcodes = hq.tile([P, CHUNK], U32, name="hcodes", tag="hcodes", align_bytes=64)
+            hscales = hq.tile([P, CHUNK], U8, name="hscales", tag="hscales", align_bytes=64)
+            nc.vector.quantize_mx(
+                out=hcodes[:].bitcast(FP8X4),
+                scales=hscales[:],
+                in_=st[("hgrp", i)][:].rearrange("p c t -> p (c t)"),
+            )
+            st[("hc", i)] = (hcodes, hscales)
+
+        def layer2(i, a):
+            b = i // NCH
+            hcodes, hscales = st[("hc", i)]
+            op = ps_o.tile([P, D], F32, name="op", tag="o")
+            nc.tensor.matmul_mx(
+                out=op[:],
+                lhsT=hcodes[:, P * a : P * (a + 1)].bitcast(FP8X4),
+                lhsT_scale=hscales[:, P * a : P * (a + 1)],
+                rhs=wcodes[:, 2 * b + 1, :].bitcast(FP8X4),
+                rhs_scale=wscales[:, 2 * b + 1, :],
+                start=True,
+                stop=True,
+            )
+            st[("op", i, a)] = op
+
+        def add(i, a):
+            b = i // NCH
+            if a == 0:
+                st[("osb", i)] = ostage.tile([P, TILES, D], F32, name="osb", tag="osb")
+            nc.vector.tensor_tensor(
+                out=st[("osb", i)][:, a, :], in0=st[("op", i, a)][:], in1=b1_bc[:, b, :], op=ALU.add
+            )
+
+        def relu(i, engine, a0, a1):
+            part = st[("osb", i)][:, a0:a1, :]
+            if engine == "S":
+                nc.scalar.activation(out=part, in_=part, func=ACT.Relu)
+            elif engine == "V":
+                nc.vector.tensor_scalar_max(out=part, in0=part, scalar1=0.0)
+            else:
+                nc.gpsimd.tensor_scalar(
+                    out=part, in0=part, scalar1=FLT_MAX, scalar2=0.0, op0=ALU.min, op1=ALU.max
+                )
+
+        def relu_store(i, half):
+            b, c = divmod(i, NCH)
+            plan = RELU_A if half == 0 else RELU_B
+            if len(plan) == 1:
+                relu(i, plan, 2 * half, 2 * half + 2)
+            else:
+                relu(i, plan[0], 2 * half, 2 * half + 1)
+                relu(i, plan[1], 2 * half + 1, 2 * half + 2)
+            dst = out[b].rearrange("(m a) e -> m a e", a=APP)
+            nc.sync.dma_start(
+                out=dst[:, TILES * c + 2 * half : TILES * c + 2 * half + 2, :],
+                in_=st[("osb", i)][:, 2 * half : 2 * half + 2, :],
+            )
+
+        regroup_w(0, 0, None)
+        transposes(0, 0)
+        transposes(0, 1)
+        b0T = ps_h.tile([P, PACK, P], BF16, name="b0T", tag="h")
+        for t in range(PACK):
+            nc.tensor.transpose(b0T[:, t, :], b0rows[:, t : D : PACK], ident_b[:])
+        b0_sb = const.tile([P, PACK, NB], F32, name="b0_sb")
+        nc.vector.tensor_copy(out=b0_sb[:], in_=b0T[:, :, 0:NB])
+        quant_w(0, 0)
+        b1_bc = const.tile([P, NB, D], F32, name="b1_bc")
+
+        def spread_b1(b):
+            bp = ps_o.tile([P, D], F32, name="bp", tag="o")
+            nc.tensor.matmul(bp[:], lhsT=ones[:], rhs=b1row[:, D * b : D * (b + 1)], start=True, stop=True)
+            nc.vector.tensor_copy(out=b1_bc[:, b, :], in_=bp[:])
+
+        def ok(i):
+            return 0 <= i < TOTAL
+
+        for j in range(TOTAL + 5):
+            if ok(j - 3):
+                add(j - 3, 0)
+            if ok(j):
+                copy_x(j, 0)
+            if ok(j - 3):
+                layer2(j - 3, 3)
+            if ok(j - 1):
+                act(j - 1, 0)
+            if ok(j + 1):
+                transposes(j + 1, 0)
+            if ok(j - 1):
+                layer1(j - 1, 3)
+            if ok(j - 2):
+                regroup_h(j - 2)
+            if ok(j):
+                copy_x(j, 1)
+            if ok(j + 1):
+                transposes(j + 1, 1)
+            if ok(j - 3):
+                add(j - 3, 1)
+            if ok(j - 1):
+                act(j - 1, 1)
+            if ok(j - 2):
+                quant_h(j - 2)
+            if ok(j - 4):
+                relu_store(j - 4, 0)
+            if ok(j - 3):
+                add(j - 3, 2)
+            if ok(j - 2):
+                layer2(j - 2, 0)
+                layer2(j - 2, 1)
+            if ok(j - 1):
+                act(j - 1, 2)
+            if ok(j):
+                quant_x(j)
+            if ok(j - 4):
+                relu_store(j - 4, 1)
+            if ok(j - 3):
+                add(j - 3, 3)
+            if ok(j):
+                layer1(j, 0)
+                layer1(j, 1)
+            if ok(j - 2):
+                layer2(j - 2, 2)
+            if ok(j - 1):
+                act(j - 1, 3)
+            if ok(j):
+                layer1(j, 2)
+            if 4 <= j < TOTAL - 4:
+                load_x(j + 4)
+                if j % NCH == 0:
+                    load_w(j // NCH + 1, 0)
+                    load_w(j // NCH + 1, 1)
+            if j == 0:
+                regroup_w(0, 1, None)
+                spread_b1(0)
+                spread_b1(1)
+            if j == 1:
+                quant_w(0, 1)
+                spread_b1(2)
+                spread_b1(3)
+            b, c = divmod(j - 1, NCH)
+            if 0 <= b and b + 1 < NB:
+                for part in range(HR_PARTS // 2):
+                    regroup_w(b + 1, c // 2, (c % 2) * (HR_PARTS // 2) + part)
+            b, c = divmod(j - 3, NCH)
+            if 0 <= b and b + 1 < NB and c % 2 == 0:
+                quant_w(b + 1, c // 2)

@@ -11,12 +11,6 @@ FP8X4 = mybir.dt.float8_e4m3fn_x4
 ACT = mybir.ActivationFunctionType
 ALU = mybir.AluOpType
 
-PINNED = True
-RELU_A = "S"
-RELU_B = "SV"
-HR = "G"
-HR_PARTS = 4
-
 P = 128
 NB = 4
 NTOK = 2048
@@ -30,7 +24,8 @@ TOTAL = NB * NCH
 OFF_W = (0, D * D + D)
 OFF_B0 = D * D
 OFF_B1 = 2 * D * D + D
-FLT_MAX = 3.4028234663852886e38
+
+RELU_ENGINE = ("G", "G", "S", "S")
 
 FLOPS = 2 * NB * NTOK * D * D * 2
 
@@ -38,10 +33,9 @@ FLOPS = 2 * NB * NTOK * D * D * 2
 def tile_can_t_kernel(tc, user_emb, item_emb, out):
     nc = tc.nc
     with ExitStack() as ctx:
-        if PINNED:
-            ctx.enter_context(tc.manual_schedule())
+        ctx.enter_context(tc.manual_schedule())
         const = ctx.enter_context(tc.tile_pool(name="const", bufs=1))
-        wstage = ctx.enter_context(tc.tile_pool(name="wstage", bufs=2))
+        wstage = ctx.enter_context(tc.tile_pool(name="wstage", bufs=4))
         xq = ctx.enter_context(tc.tile_pool(name="xq", bufs=2))
         hstage = ctx.enter_context(tc.tile_pool(name="hstage", bufs=2))
         hq = ctx.enter_context(tc.tile_pool(name="hq", bufs=2))
@@ -81,12 +75,16 @@ def tile_can_t_kernel(tc, user_emb, item_emb, out):
             in_=item_emb[:, OFF_B1 : OFF_B1 + D].unsqueeze(0),
         )
         load_w(0, 1)
-        for i in range(1, 5):
-            load_x(i)
+        load_x(1)
         load_w(1, 0)
+        load_x(2)
         load_w(1, 1)
-        for i in range(5, 8):
-            load_x(i)
+        load_x(3)
+        load_w(2, 0)
+        load_x(4)
+        load_w(2, 1)
+        load_x(5)
+        load_x(6)
 
         ident_f = const.tile([P, P], F32, name="ident_f")
         make_identity(nc, ident_f[:])
@@ -97,33 +95,18 @@ def tile_can_t_kernel(tc, user_emb, item_emb, out):
         wscales = const.tile([P, 2 * NB, D], U8, name="wscales", align_bytes=64)
         wgrp = {}
 
-        def regroup_w(b, layer, part):
-            if part is None or part == 0:
+        def regroup_w(b, layer, piece, engine):
+            if piece == 0:
                 wgrp[(b, layer)] = wstage.tile([P, D, PACK], BF16, name="wgrp", tag="wgrp", align_bytes=64)
+            dst = wgrp[(b, layer)][:].rearrange("p (q c i) j -> p q c j i", q=PACK, i=4)[:, piece]
             if layer == 0:
-                dst = wgrp[(b, layer)][:].rearrange("p (t c i) j -> p t c j i", t=PACK, i=4)
-                src = wraw[(b, layer)][:].rearrange("p j (c i t) -> p t c j i", t=PACK, i=4)
-                pieces = [(dst[:, t], src[:, t]) for t in range(PACK)]
+                src = wraw[(b, layer)][:].rearrange("p j (c i q) -> p q c j i", q=PACK, i=4)[:, piece]
             else:
-                dst = wgrp[(b, layer)][:].rearrange("p (q c i) j -> p q c j i", q=HR_PARTS, i=4)
-                src = wraw[(b, layer)][:].rearrange("p j (q c i) -> p q c j i", q=HR_PARTS, i=4)
-                pieces = [(dst[:, t], src[:, t]) for t in range(PACK)]
-            if part is None:
-                for piece_dst, piece_src in pieces:
-                    nc.vector.tensor_copy(out=piece_dst, in_=piece_src)
-                return
-            piece_dst, piece_src = pieces[part]
-            if HR == "S":
-                nc.scalar.copy(out=piece_dst, in_=piece_src)
+                src = wraw[(b, layer)][:].rearrange("p j (q c i) -> p q c j i", q=PACK, i=4)[:, piece]
+            if engine == "V":
+                nc.vector.tensor_copy(out=dst, in_=src)
             else:
-                nc.gpsimd.tensor_scalar(
-                    out=piece_dst,
-                    in0=piece_src,
-                    scalar1=1.0,
-                    scalar2=0.0,
-                    op0=ALU.mult,
-                    op1=ALU.add,
-                )
+                nc.gpsimd.tensor_scalar(out=dst, in0=src, scalar1=1.0, scalar2=0.0, op0=ALU.mult, op1=ALU.add)
 
         def quant_w(b, layer):
             j = 2 * b + layer
@@ -226,116 +209,116 @@ def tile_can_t_kernel(tc, user_emb, item_emb, out):
                 out=st[("osb", i)][:, a, :], in0=st[("op", i, a)][:], in1=b1_bc[:, b, :], op=ALU.add
             )
 
-        def relu(i, engine, a0, a1):
-            part = st[("osb", i)][:, a0:a1, :]
-            if engine == "S":
+        def relu(i, a):
+            part = st[("osb", i)][:, a, :]
+            if RELU_ENGINE[a] == "S":
                 nc.scalar.activation(out=part, in_=part, func=ACT.Relu)
-            elif engine == "V":
-                nc.vector.tensor_scalar_max(out=part, in0=part, scalar1=0.0)
             else:
-                nc.gpsimd.tensor_scalar(
-                    out=part, in0=part, scalar1=FLT_MAX, scalar2=0.0, op0=ALU.min, op1=ALU.max
-                )
+                nc.gpsimd.tensor_scalar(out=part, in0=part, scalar1=0.0, scalar2=0.0, op0=ALU.max, op1=ALU.max)
 
-        def relu_store(i, half):
+        def store(i, half):
             b, c = divmod(i, NCH)
-            plan = RELU_A if half == 0 else RELU_B
-            if len(plan) == 1:
-                relu(i, plan, 2 * half, 2 * half + 2)
-            else:
-                relu(i, plan[0], 2 * half, 2 * half + 1)
-                relu(i, plan[1], 2 * half + 1, 2 * half + 2)
             dst = out[b].rearrange("(m a) e -> m a e", a=APP)
             nc.sync.dma_start(
                 out=dst[:, TILES * c + 2 * half : TILES * c + 2 * half + 2, :],
                 in_=st[("osb", i)][:, 2 * half : 2 * half + 2, :],
             )
 
-        regroup_w(0, 0, None)
+        for q in range(PACK):
+            regroup_w(0, 0, q, "V")
         transposes(0, 0)
         transposes(0, 1)
         b0T = ps_h.tile([P, PACK, P], BF16, name="b0T", tag="h")
         for t in range(PACK):
             nc.tensor.transpose(b0T[:, t, :], b0rows[:, t : D : PACK], ident_b[:])
         b0_sb = const.tile([P, PACK, NB], F32, name="b0_sb")
-        nc.vector.tensor_copy(out=b0_sb[:], in_=b0T[:, :, 0:NB])
         quant_w(0, 0)
         b1_bc = const.tile([P, NB, D], F32, name="b1_bc")
 
         def spread_b1(b):
             bp = ps_o.tile([P, D], F32, name="bp", tag="o")
             nc.tensor.matmul(bp[:], lhsT=ones[:], rhs=b1row[:, D * b : D * (b + 1)], start=True, stop=True)
-            nc.vector.tensor_copy(out=b1_bc[:, b, :], in_=bp[:])
+            nc.scalar.copy(out=b1_bc[:, b, :], in_=bp[:])
 
         def ok(i):
             return 0 <= i < TOTAL
 
-        for j in range(TOTAL + 5):
-            if ok(j - 3):
-                add(j - 3, 0)
+        pieces = [(b, layer, q) for b in (2, 3) for layer in (0, 1) for q in range(PACK)]
+        piece_slots = [2 + n // 2 for n in range(8)] + [6 + n for n in range(8)]
+        quant_slots = {(2, 0): 4, (2, 1): 6, (3, 0): 10, (3, 1): 14}
+
+        for j in range(TOTAL + 3):
             if ok(j):
                 copy_x(j, 0)
-            if ok(j - 3):
-                layer2(j - 3, 3)
-            if ok(j - 1):
-                act(j - 1, 0)
-            if ok(j + 1):
-                transposes(j + 1, 0)
-            if ok(j - 1):
-                layer1(j - 1, 3)
+                copy_x(j, 1)
+            if j == 0:
+                nc.scalar.copy(out=b0_sb[:], in_=b0T[:, :, 0:NB])
             if ok(j - 2):
                 regroup_h(j - 2)
-            if ok(j):
-                copy_x(j, 1)
-            if ok(j + 1):
-                transposes(j + 1, 1)
+            if ok(j - 1):
+                act(j - 1, 0)
             if ok(j - 3):
+                add(j - 3, 0)
+            if ok(j + 1):
+                transposes(j + 1, 0)
+                transposes(j + 1, 1)
+            if ok(j - 1):
+                layer1(j - 1, 3)
+            if ok(j - 3):
+                layer2(j - 3, 3)
+                relu(j - 3, 0)
                 add(j - 3, 1)
+                relu(j - 3, 1)
             if ok(j - 1):
                 act(j - 1, 1)
-            if ok(j - 2):
-                quant_h(j - 2)
-            if ok(j - 4):
-                relu_store(j - 4, 0)
             if ok(j - 3):
+                store(j - 3, 0)
                 add(j - 3, 2)
-            if ok(j - 2):
-                layer2(j - 2, 0)
-                layer2(j - 2, 1)
+                add(j - 3, 3)
             if ok(j - 1):
                 act(j - 1, 2)
+                act(j - 1, 3)
+            for piece, slot in zip(pieces, piece_slots):
+                if slot == j:
+                    regroup_w(piece[0], piece[1], piece[2], "G")
+            for b, layer in quant_slots:
+                if quant_slots[(b, layer)] == j:
+                    quant_w(b, layer)
             if ok(j):
                 quant_x(j)
-            if ok(j - 4):
-                relu_store(j - 4, 1)
             if ok(j - 3):
-                add(j - 3, 3)
+                relu(j - 3, 2)
+                relu(j - 3, 3)
+                store(j - 3, 1)
             if ok(j):
                 layer1(j, 0)
                 layer1(j, 1)
-            if ok(j - 2):
-                layer2(j - 2, 2)
-            if ok(j - 1):
-                act(j - 1, 3)
-            if ok(j):
                 layer1(j, 2)
-            if 4 <= j < TOTAL - 4:
-                load_x(j + 4)
-                if j % NCH == 0:
-                    load_w(j // NCH + 1, 0)
-                    load_w(j // NCH + 1, 1)
             if j == 0:
-                regroup_w(0, 1, None)
+                for q in range(PACK):
+                    regroup_w(0, 1, q, "V")
                 spread_b1(0)
                 spread_b1(1)
             if j == 1:
                 quant_w(0, 1)
                 spread_b1(2)
                 spread_b1(3)
-            b, c = divmod(j - 1, NCH)
-            if 0 <= b and b + 1 < NB:
-                for part in range(HR_PARTS // 2):
-                    regroup_w(b + 1, c // 2, (c % 2) * (HR_PARTS // 2) + part)
-            b, c = divmod(j - 3, NCH)
-            if 0 <= b and b + 1 < NB and c % 2 == 0:
-                quant_w(b + 1, c // 2)
+                for q in range(PACK):
+                    regroup_w(1, 0, q, "V")
+            if ok(j - 2):
+                quant_h(j - 2)
+                layer2(j - 2, 0)
+                layer2(j - 2, 1)
+                layer2(j - 2, 2)
+            if j == 2:
+                quant_w(1, 0)
+                for q in range(PACK):
+                    regroup_w(1, 1, q, "V")
+            if j == 3:
+                quant_w(1, 1)
+            if 2 <= j < TOTAL - 5:
+                load_x(j + 5)
+                if j == 3:
+                    load_w(3, 0)
+                if j == 5:
+                    load_w(3, 1)

@@ -25,8 +25,6 @@ OFF_W = (0, D * D + D)
 OFF_B0 = D * D
 OFF_B1 = 2 * D * D + D
 
-RELU_ENGINE = ("G", "G", "S", "S")
-
 FLOPS = 2 * NB * NTOK * D * D * 2
 
 
@@ -60,20 +58,20 @@ def tile_can_t_kernel(tc, user_emb, item_emb, out):
             nc.sync.dma_start(out=t[:], in_=src[:, TILES * c : TILES * (c + 1), :])
             xraw[i] = t
 
-        b0rows = const.tile([P, D], BF16, name="b0rows")
-        nc.vector.memset(b0rows[:], 0.0)
         b1row = const.tile([P, NB * D], BF16, name="b1row")
         nc.vector.memset(b1row[:], 0.0)
+        b0rows = const.tile([P, D], BF16, name="b0rows")
+        nc.vector.memset(b0rows[:], 0.0)
         ones = const.tile([P, P], BF16, name="ones")
         nc.vector.memset(ones[:], 1.0)
 
         load_w(0, 0)
-        load_x(0)
-        nc.sync.dma_start(out=b0rows[0:NB, :], in_=item_emb[:, OFF_B0 : OFF_B0 + D])
         nc.sync.dma_start(
             out=b1row[0:1, :].rearrange("o (b e) -> o b e", b=NB),
             in_=item_emb[:, OFF_B1 : OFF_B1 + D].unsqueeze(0),
         )
+        nc.sync.dma_start(out=b0rows[0:NB, :], in_=item_emb[:, OFF_B0 : OFF_B0 + D])
+        load_x(0)
         load_w(0, 1)
         load_x(1)
         load_w(1, 0)
@@ -95,7 +93,7 @@ def tile_can_t_kernel(tc, user_emb, item_emb, out):
         wscales = const.tile([P, 2 * NB, D], U8, name="wscales", align_bytes=64)
         wgrp = {}
 
-        def regroup_w(b, layer, piece, engine):
+        def regroup_w(b, layer, piece):
             if piece == 0:
                 wgrp[(b, layer)] = wstage.tile([P, D, PACK], BF16, name="wgrp", tag="wgrp", align_bytes=64)
             dst = wgrp[(b, layer)][:].rearrange("p (q c i) j -> p q c j i", q=PACK, i=4)[:, piece]
@@ -103,10 +101,7 @@ def tile_can_t_kernel(tc, user_emb, item_emb, out):
                 src = wraw[(b, layer)][:].rearrange("p j (c i q) -> p q c j i", q=PACK, i=4)[:, piece]
             else:
                 src = wraw[(b, layer)][:].rearrange("p j (q c i) -> p q c j i", q=PACK, i=4)[:, piece]
-            if engine == "V":
-                nc.vector.tensor_copy(out=dst, in_=src)
-            else:
-                nc.gpsimd.tensor_scalar(out=dst, in0=src, scalar1=1.0, scalar2=0.0, op0=ALU.mult, op1=ALU.add)
+            nc.vector.tensor_copy(out=dst, in_=src)
 
         def quant_w(b, layer):
             j = 2 * b + layer
@@ -209,12 +204,12 @@ def tile_can_t_kernel(tc, user_emb, item_emb, out):
                 out=st[("osb", i)][:, a, :], in0=st[("op", i, a)][:], in1=b1_bc[:, b, :], op=ALU.add
             )
 
-        def relu(i, a):
+        def relu(i, a, engine):
             part = st[("osb", i)][:, a, :]
-            if RELU_ENGINE[a] == "S":
+            if engine == "S":
                 nc.scalar.activation(out=part, in_=part, func=ACT.Relu)
             else:
-                nc.gpsimd.tensor_scalar(out=part, in0=part, scalar1=0.0, scalar2=0.0, op0=ALU.max, op1=ALU.max)
+                nc.vector.tensor_scalar_max(out=part, in0=part, scalar1=0.0)
 
         def store(i, half):
             b, c = divmod(i, NCH)
@@ -224,15 +219,8 @@ def tile_can_t_kernel(tc, user_emb, item_emb, out):
                 in_=st[("osb", i)][:, 2 * half : 2 * half + 2, :],
             )
 
-        for q in range(PACK):
-            regroup_w(0, 0, q, "V")
-        transposes(0, 0)
-        transposes(0, 1)
         b0T = ps_h.tile([P, PACK, P], BF16, name="b0T", tag="h")
-        for t in range(PACK):
-            nc.tensor.transpose(b0T[:, t, :], b0rows[:, t : D : PACK], ident_b[:])
         b0_sb = const.tile([P, PACK, NB], F32, name="b0_sb")
-        quant_w(0, 0)
         b1_bc = const.tile([P, NB, D], F32, name="b1_bc")
 
         def spread_b1(b):
@@ -240,81 +228,81 @@ def tile_can_t_kernel(tc, user_emb, item_emb, out):
             nc.tensor.matmul(bp[:], lhsT=ones[:], rhs=b1row[:, D * b : D * (b + 1)], start=True, stop=True)
             nc.scalar.copy(out=b1_bc[:, b, :], in_=bp[:])
 
+        def regroup(b, layer):
+            for q in range(PACK):
+                regroup_w(b, layer, q)
+
+        for b in range(NB):
+            spread_b1(b)
+        for t in range(PACK):
+            nc.tensor.transpose(b0T[:, t, :], b0rows[:, t : D : PACK], ident_b[:])
+        nc.scalar.copy(out=b0_sb[:], in_=b0T[:, :, 0:NB])
+        regroup(0, 0)
+        transposes(0, 0)
+        transposes(0, 1)
+        quant_w(0, 0)
+        regroup(0, 1)
+
         def ok(i):
             return 0 <= i < TOTAL
 
-        pieces = [(b, layer, q) for b in (2, 3) for layer in (0, 1) for q in range(PACK)]
-        piece_slots = [2 + n // 2 for n in range(8)] + [6 + n for n in range(8)]
-        quant_slots = {(2, 0): 4, (2, 1): 6, (3, 0): 10, (3, 1): 14}
+        regroup_slots = {(2, 0): 4, (2, 1): 6, (3, 0): 8, (3, 1): 10}
 
         for j in range(TOTAL + 3):
             if ok(j):
                 copy_x(j, 0)
+            if ok(j - 3):
+                add(j - 3, 0)
+                layer2(j - 3, 3)
+            if ok(j):
                 copy_x(j, 1)
-            if j == 0:
-                nc.scalar.copy(out=b0_sb[:], in_=b0T[:, :, 0:NB])
+            if ok(j + 1):
+                transposes(j + 1, 0)
+                transposes(j + 1, 1)
+            if ok(j - 3):
+                add(j - 3, 1)
             if ok(j - 2):
                 regroup_h(j - 2)
             if ok(j - 1):
                 act(j - 1, 0)
-            if ok(j - 3):
-                add(j - 3, 0)
-            if ok(j + 1):
-                transposes(j + 1, 0)
-                transposes(j + 1, 1)
-            if ok(j - 1):
                 layer1(j - 1, 3)
             if ok(j - 3):
-                layer2(j - 3, 3)
-                relu(j - 3, 0)
-                add(j - 3, 1)
-                relu(j - 3, 1)
-            if ok(j - 1):
-                act(j - 1, 1)
-            if ok(j - 3):
-                store(j - 3, 0)
                 add(j - 3, 2)
                 add(j - 3, 3)
             if ok(j - 1):
+                act(j - 1, 1)
                 act(j - 1, 2)
                 act(j - 1, 3)
-            for piece, slot in zip(pieces, piece_slots):
-                if slot == j:
-                    regroup_w(piece[0], piece[1], piece[2], "G")
-            for b, layer in quant_slots:
-                if quant_slots[(b, layer)] == j:
-                    quant_w(b, layer)
-            if ok(j):
-                quant_x(j)
             if ok(j - 3):
-                relu(j - 3, 2)
-                relu(j - 3, 3)
+                relu(j - 3, 0, "S" if 6 <= j <= 12 else "V")
+                for a in range(1, TILES):
+                    relu(j - 3, a, "S")
+                store(j - 3, 0)
                 store(j - 3, 1)
-            if ok(j):
-                layer1(j, 0)
-                layer1(j, 1)
-                layer1(j, 2)
-            if j == 0:
-                for q in range(PACK):
-                    regroup_w(0, 1, q, "V")
-                spread_b1(0)
-                spread_b1(1)
-            if j == 1:
-                quant_w(0, 1)
-                spread_b1(2)
-                spread_b1(3)
-                for q in range(PACK):
-                    regroup_w(1, 0, q, "V")
+            for b, layer in regroup_slots:
+                first = regroup_slots[(b, layer)]
+                if j in (first, first + 1):
+                    regroup_w(b, layer, 2 * (j - first))
+                    regroup_w(b, layer, 2 * (j - first) + 1)
+                if j == first + 2:
+                    quant_w(b, layer)
             if ok(j - 2):
                 quant_h(j - 2)
                 layer2(j - 2, 0)
                 layer2(j - 2, 1)
                 layer2(j - 2, 2)
-            if j == 2:
+            if ok(j):
+                quant_x(j)
+                layer1(j, 0)
+                layer1(j, 1)
+                layer1(j, 2)
+            if j == 0:
+                quant_w(0, 1)
+                regroup(1, 0)
+            if j == 1:
                 quant_w(1, 0)
-                for q in range(PACK):
-                    regroup_w(1, 1, q, "V")
-            if j == 3:
+                regroup(1, 1)
+            if j == 2:
                 quant_w(1, 1)
             if 2 <= j < TOTAL - 5:
                 load_x(j + 5)

@@ -24,6 +24,7 @@ TOTAL = NB * NCH
 OFF_W = (0, D * D + D)
 OFF_B0 = D * D
 OFF_B1 = 2 * D * D + D
+FLT_MAX = 3.4028234663852886e38
 
 FLOPS = 2 * NB * NTOK * D * D * 2
 
@@ -66,12 +67,12 @@ def tile_can_t_kernel(tc, user_emb, item_emb, out):
         nc.vector.memset(ones[:], 1.0)
 
         load_w(0, 0)
+        load_x(0)
+        nc.sync.dma_start(out=b0rows[0:NB, :], in_=item_emb[:, OFF_B0 : OFF_B0 + D])
         nc.sync.dma_start(
             out=b1row[0:1, :].rearrange("o (b e) -> o b e", b=NB),
             in_=item_emb[:, OFF_B1 : OFF_B1 + D].unsqueeze(0),
         )
-        nc.sync.dma_start(out=b0rows[0:NB, :], in_=item_emb[:, OFF_B0 : OFF_B0 + D])
-        load_x(0)
         load_w(0, 1)
         load_x(1)
         load_w(1, 0)
@@ -201,15 +202,17 @@ def tile_can_t_kernel(tc, user_emb, item_emb, out):
             if a == 0:
                 st[("osb", i)] = ostage.tile([P, TILES, D], F32, name="osb", tag="osb")
             nc.vector.tensor_tensor(
-                out=st[("osb", i)][:, a, :], in0=st[("op", i, a)][:], in1=b1_bc[:, b, :], op=ALU.add
+                out=st[("osb", i)][:, a, :], in0=b1_bc[:, b, :], in1=st[("op", i, a)][:], op=ALU.add
             )
 
         def relu(i, a, engine):
             part = st[("osb", i)][:, a, :]
             if engine == "S":
                 nc.scalar.activation(out=part, in_=part, func=ACT.Relu)
-            else:
+            elif engine == "V":
                 nc.vector.tensor_scalar_max(out=part, in0=part, scalar1=0.0)
+            else:
+                nc.gpsimd.tensor_scalar(out=part, in0=part, scalar1=FLT_MAX, scalar2=0.0, op0=ALU.min, op1=ALU.max)
 
         def store(i, half):
             b, c = divmod(i, NCH)
@@ -232,14 +235,11 @@ def tile_can_t_kernel(tc, user_emb, item_emb, out):
             for q in range(PACK):
                 regroup_w(b, layer, q)
 
-        for b in range(NB):
-            spread_b1(b)
-        for t in range(PACK):
-            nc.tensor.transpose(b0T[:, t, :], b0rows[:, t : D : PACK], ident_b[:])
-        nc.scalar.copy(out=b0_sb[:], in_=b0T[:, :, 0:NB])
         regroup(0, 0)
         transposes(0, 0)
         transposes(0, 1)
+        for t in range(PACK):
+            nc.tensor.transpose(b0T[:, t, :], b0rows[:, t : D : PACK], ident_b[:])
         quant_w(0, 0)
         regroup(0, 1)
 
@@ -247,37 +247,44 @@ def tile_can_t_kernel(tc, user_emb, item_emb, out):
             return 0 <= i < TOTAL
 
         regroup_slots = {(2, 0): 4, (2, 1): 6, (3, 0): 8, (3, 1): 10}
+        relu_engine = ("G", "G", "S", "S")
 
         for j in range(TOTAL + 3):
             if ok(j):
                 copy_x(j, 0)
+                copy_x(j, 1)
+            if j == 0:
+                nc.scalar.copy(out=b0_sb[:], in_=b0T[:, :, 0:NB])
+                spread_b1(0)
+            if j == 1:
+                spread_b1(1)
+            if j == 2:
+                spread_b1(2)
+                spread_b1(3)
+            if ok(j - 2):
+                regroup_h(j - 2)
             if ok(j - 3):
                 add(j - 3, 0)
                 layer2(j - 3, 3)
-            if ok(j):
-                copy_x(j, 1)
+                relu(j - 3, 0, relu_engine[0])
+                add(j - 3, 1)
+                relu(j - 3, 1, relu_engine[1])
+                store(j - 3, 0)
             if ok(j + 1):
                 transposes(j + 1, 0)
                 transposes(j + 1, 1)
             if ok(j - 3):
-                add(j - 3, 1)
-            if ok(j - 2):
-                regroup_h(j - 2)
-            if ok(j - 1):
-                act(j - 1, 0)
-                layer1(j - 1, 3)
-            if ok(j - 3):
                 add(j - 3, 2)
                 add(j - 3, 3)
             if ok(j - 1):
+                act(j - 1, 0)
+                layer1(j - 1, 3)
                 act(j - 1, 1)
                 act(j - 1, 2)
                 act(j - 1, 3)
             if ok(j - 3):
-                relu(j - 3, 0, "S" if 6 <= j <= 12 else "V")
-                for a in range(1, TILES):
-                    relu(j - 3, a, "S")
-                store(j - 3, 0)
+                relu(j - 3, 2, relu_engine[2])
+                relu(j - 3, 3, relu_engine[3])
                 store(j - 3, 1)
             for b, layer in regroup_slots:
                 first = regroup_slots[(b, layer)]
@@ -286,16 +293,16 @@ def tile_can_t_kernel(tc, user_emb, item_emb, out):
                     regroup_w(b, layer, 2 * (j - first) + 1)
                 if j == first + 2:
                     quant_w(b, layer)
-            if ok(j - 2):
-                quant_h(j - 2)
-                layer2(j - 2, 0)
-                layer2(j - 2, 1)
-                layer2(j - 2, 2)
             if ok(j):
                 quant_x(j)
                 layer1(j, 0)
                 layer1(j, 1)
                 layer1(j, 2)
+            if ok(j - 2):
+                quant_h(j - 2)
+                layer2(j - 2, 0)
+                layer2(j - 2, 1)
+                layer2(j - 2, 2)
             if j == 0:
                 quant_w(0, 1)
                 regroup(1, 0)

@@ -34,8 +34,8 @@ def tile_can_t_kernel(tc, user_emb, item_emb, out):
     with ExitStack() as ctx:
         ctx.enter_context(tc.manual_schedule())
         const = ctx.enter_context(tc.tile_pool(name="const", bufs=1))
-        wstage = ctx.enter_context(tc.tile_pool(name="wstage", bufs=4))
-        xq = ctx.enter_context(tc.tile_pool(name="xq", bufs=2))
+        wstage = ctx.enter_context(tc.tile_pool(name="wstage", bufs=3))
+        xq = ctx.enter_context(tc.tile_pool(name="xq", bufs=3))
         hstage = ctx.enter_context(tc.tile_pool(name="hstage", bufs=2))
         hq = ctx.enter_context(tc.tile_pool(name="hq", bufs=2))
         ostage = ctx.enter_context(tc.tile_pool(name="ostage", bufs=4))
@@ -59,50 +59,47 @@ def tile_can_t_kernel(tc, user_emb, item_emb, out):
             nc.sync.dma_start(out=t[:], in_=src[:, TILES * c : TILES * (c + 1), :])
             xraw[i] = t
 
-        b1row = const.tile([P, NB * D], BF16, name="b1row")
-        nc.vector.memset(b1row[:], 0.0)
-        b0rows = const.tile([P, D], BF16, name="b0rows")
-        nc.vector.memset(b0rows[:], 0.0)
-        ones = const.tile([P, P], BF16, name="ones")
-        nc.vector.memset(ones[:], 1.0)
+        b0_sb = const.tile([P, NB, PACK], BF16, name="b0_sb")
+        b1_bc = const.tile([P, NB, D], BF16, name="b1_bc")
+
+        def load_b1(b):
+            nc.sync.dma_start(out=b1_bc[:, b, :], in_=item_emb[b, OFF_B1 : OFF_B1 + D].partition_broadcast(P))
 
         load_w(0, 0)
         load_x(0)
-        nc.sync.dma_start(out=b0rows[0:NB, :], in_=item_emb[:, OFF_B0 : OFF_B0 + D])
         nc.sync.dma_start(
-            out=b1row[0:1, :].rearrange("o (b e) -> o b e", b=NB),
-            in_=item_emb[:, OFF_B1 : OFF_B1 + D].unsqueeze(0),
+            out=b0_sb[:], in_=item_emb[:, OFF_B0 : OFF_B0 + D].rearrange("b (p t) -> p b t", t=PACK)
         )
         load_w(0, 1)
         load_x(1)
         load_w(1, 0)
-        load_x(2)
         load_w(1, 1)
-        load_x(3)
+        load_x(2)
+        load_b1(0)
         load_w(2, 0)
-        load_x(4)
+        load_x(3)
         load_w(2, 1)
+        load_x(4)
         load_x(5)
         load_x(6)
 
         ident_f = const.tile([P, P], F32, name="ident_f")
         make_identity(nc, ident_f[:])
-        ident_b = const.tile([P, P], BF16, name="ident_b")
-        make_identity(nc, ident_b[:])
 
         wcodes = const.tile([P, 2 * NB, D], U32, name="wcodes", align_bytes=64)
         wscales = const.tile([P, 2 * NB, D], U8, name="wscales", align_bytes=64)
         wgrp = {}
 
-        def regroup_w(b, layer, piece):
-            if piece == 0:
-                wgrp[(b, layer)] = wstage.tile([P, D, PACK], BF16, name="wgrp", tag="wgrp", align_bytes=64)
-            dst = wgrp[(b, layer)][:].rearrange("p (q c i) j -> p q c j i", q=PACK, i=4)[:, piece]
+        def regroup_w(b, layer):
+            grp = wstage.tile([P, D, PACK], BF16, name="wgrp", tag="wgrp", align_bytes=64)
             if layer == 0:
-                src = wraw[(b, layer)][:].rearrange("p j (c i q) -> p q c j i", q=PACK, i=4)[:, piece]
+                dst = grp[:].rearrange("p (t m) j -> p m j t", t=PACK)
+                src = wraw[(b, layer)][:].rearrange("p j (m t) -> p m j t", t=PACK)
             else:
-                src = wraw[(b, layer)][:].rearrange("p j (q c i) -> p q c j i", q=PACK, i=4)[:, piece]
+                dst = grp[:].rearrange("p (c i) j -> p c j i", i=4)
+                src = wraw[(b, layer)][:].rearrange("p j (c i) -> p c j i", i=4)
             nc.vector.tensor_copy(out=dst, in_=src)
+            wgrp[(b, layer)] = grp
 
         def quant_w(b, layer):
             j = 2 * b + layer
@@ -154,13 +151,13 @@ def tile_can_t_kernel(tc, user_emb, item_emb, out):
 
         def act(i, t):
             b = i // NCH
-            if t == 0:
+            if ("hT", i) not in st:
                 st[("hT", i)] = hstage.tile([P, PACK, CHUNK], BF16, name="hT", tag="hT")
             nc.scalar.activation(
                 out=st[("hT", i)][:, t, :],
                 in_=st[("hp", i, t)][:],
                 func=ACT.Relu,
-                bias=b0_sb[:, t, b : b + 1],
+                bias=b0_sb[:, b, t : t + 1],
                 scale=1.0,
             )
 
@@ -202,11 +199,11 @@ def tile_can_t_kernel(tc, user_emb, item_emb, out):
             if a == 0:
                 st[("osb", i)] = ostage.tile([P, TILES, D], F32, name="osb", tag="osb")
             nc.vector.tensor_tensor(
-                out=st[("osb", i)][:, a, :], in0=b1_bc[:, b, :], in1=st[("op", i, a)][:], op=ALU.add
+                out=st[("osb", i)][:, a, :], in0=st[("op", i, a)][:], in1=b1_bc[:, b, :], op=ALU.add
             )
 
-        def relu(i, a, engine):
-            part = st[("osb", i)][:, a, :]
+        def relu(i, a0, a1, engine):
+            part = st[("osb", i)][:, a0:a1, :]
             if engine == "S":
                 nc.scalar.activation(out=part, in_=part, func=ACT.Relu)
             elif engine == "V":
@@ -214,106 +211,80 @@ def tile_can_t_kernel(tc, user_emb, item_emb, out):
             else:
                 nc.gpsimd.tensor_scalar(out=part, in0=part, scalar1=FLT_MAX, scalar2=0.0, op0=ALU.min, op1=ALU.max)
 
-        def store(i, half):
+        def store(i, a0, a1):
             b, c = divmod(i, NCH)
             dst = out[b].rearrange("(m a) e -> m a e", a=APP)
-            nc.sync.dma_start(
-                out=dst[:, TILES * c + 2 * half : TILES * c + 2 * half + 2, :],
-                in_=st[("osb", i)][:, 2 * half : 2 * half + 2, :],
-            )
-
-        b0T = ps_h.tile([P, PACK, P], BF16, name="b0T", tag="h")
-        b0_sb = const.tile([P, PACK, NB], F32, name="b0_sb")
-        b1_bc = const.tile([P, NB, D], F32, name="b1_bc")
-
-        def spread_b1(b):
-            bp = ps_o.tile([P, D], F32, name="bp", tag="o")
-            nc.tensor.matmul(bp[:], lhsT=ones[:], rhs=b1row[:, D * b : D * (b + 1)], start=True, stop=True)
-            nc.scalar.copy(out=b1_bc[:, b, :], in_=bp[:])
-
-        def regroup(b, layer):
-            for q in range(PACK):
-                regroup_w(b, layer, q)
-
-        regroup(0, 0)
-        transposes(0, 0)
-        transposes(0, 1)
-        for t in range(PACK):
-            nc.tensor.transpose(b0T[:, t, :], b0rows[:, t : D : PACK], ident_b[:])
-        quant_w(0, 0)
-        regroup(0, 1)
+            nc.sync.dma_start(out=dst[:, TILES * c + a0 : TILES * c + a1, :], in_=st[("osb", i)][:, a0:a1, :])
 
         def ok(i):
             return 0 <= i < TOTAL
 
-        regroup_slots = {(2, 0): 4, (2, 1): 6, (3, 0): 8, (3, 1): 10}
-        relu_engine = ("G", "G", "S", "S")
+        weight_work = {
+            -1: [(regroup_w, 0, 0), (quant_w, 0, 0), (regroup_w, 0, 1)],
+            1: [(quant_w, 0, 1), (regroup_w, 1, 0), (quant_w, 1, 0), (regroup_w, 1, 1)],
+            2: [(quant_w, 1, 1), (regroup_w, 2, 0)],
+            4: [(quant_w, 2, 0), (regroup_w, 2, 1)],
+            6: [(quant_w, 2, 1), (regroup_w, 3, 0)],
+            8: [(quant_w, 3, 0), (regroup_w, 3, 1)],
+            10: [(quant_w, 3, 1)],
+        }
 
-        for j in range(TOTAL + 3):
+        for j in range(-1, TOTAL + 3):
             if ok(j):
                 copy_x(j, 0)
                 copy_x(j, 1)
-            if j == 0:
-                nc.scalar.copy(out=b0_sb[:], in_=b0T[:, :, 0:NB])
-                spread_b1(0)
-            if j == 1:
-                spread_b1(1)
-            if j == 2:
-                spread_b1(2)
-                spread_b1(3)
             if ok(j - 2):
                 regroup_h(j - 2)
             if ok(j - 3):
                 add(j - 3, 0)
                 layer2(j - 3, 3)
-                relu(j - 3, 0, relu_engine[0])
-                add(j - 3, 1)
-                relu(j - 3, 1, relu_engine[1])
-                store(j - 3, 0)
-            if ok(j + 1):
-                transposes(j + 1, 0)
-                transposes(j + 1, 1)
-            if ok(j - 3):
-                add(j - 3, 2)
-                add(j - 3, 3)
+                if j - 3 < TOTAL - 1:
+                    relu(j - 3, 0, 1, "G")
             if ok(j - 1):
+                act(j - 1, 2)
                 act(j - 1, 0)
                 layer1(j - 1, 3)
                 act(j - 1, 1)
-                act(j - 1, 2)
                 act(j - 1, 3)
+            if ok(j - 4) and j - 4 < TOTAL - 1:
+                relu(j - 4, 1, 4, "S")
+                store(j - 4, 0, 2)
+                store(j - 4, 2, 4)
+            if ok(j + 1):
+                transposes(j + 1, 0)
+                transposes(j + 1, 1)
+            if ok(j - 2):
+                quant_h(j - 2)
             if ok(j - 3):
-                relu(j - 3, 2, relu_engine[2])
-                relu(j - 3, 3, relu_engine[3])
-                store(j - 3, 1)
-            for b, layer in regroup_slots:
-                first = regroup_slots[(b, layer)]
-                if j in (first, first + 1):
-                    regroup_w(b, layer, 2 * (j - first))
-                    regroup_w(b, layer, 2 * (j - first) + 1)
-                if j == first + 2:
-                    quant_w(b, layer)
+                add(j - 3, 3)
+                add(j - 3, 1)
+                add(j - 3, 2)
+            if j - 3 == TOTAL - 1:
+                relu(j - 3, 0, 1, "S")
+                relu(j - 3, 3, 4, "S")
+                relu(j - 3, 1, 3, "V")
+                store(j - 3, 0, 2)
+                store(j - 3, 2, 4)
+            for step, b, layer in weight_work.get(j, []):
+                step(b, layer)
+            if ok(j - 2):
+                layer2(j - 2, 0)
+                layer2(j - 2, 1)
+                layer2(j - 2, 2)
             if ok(j):
                 quant_x(j)
                 layer1(j, 0)
                 layer1(j, 1)
                 layer1(j, 2)
-            if ok(j - 2):
-                quant_h(j - 2)
-                layer2(j - 2, 0)
-                layer2(j - 2, 1)
-                layer2(j - 2, 2)
-            if j == 0:
-                quant_w(0, 1)
-                regroup(1, 0)
-            if j == 1:
-                quant_w(1, 0)
-                regroup(1, 1)
-            if j == 2:
-                quant_w(1, 1)
             if 2 <= j < TOTAL - 5:
                 load_x(j + 5)
+                if j == 2:
+                    load_b1(1)
                 if j == 3:
                     load_w(3, 0)
+                if j == 4:
+                    load_b1(2)
                 if j == 5:
                     load_w(3, 1)
+                if j == 6:
+                    load_b1(3)

@@ -221,61 +221,72 @@ def tile_can_t_kernel(tc, user_emb, item_emb, out):
 
         weight_work = {
             -1: [(regroup_w, 0, 0), (quant_w, 0, 0), (regroup_w, 0, 1)],
-            1: [(quant_w, 0, 1), (regroup_w, 1, 0), (quant_w, 1, 0), (regroup_w, 1, 1)],
-            2: [(quant_w, 1, 1), (regroup_w, 2, 0)],
-            4: [(quant_w, 2, 0), (regroup_w, 2, 1)],
-            6: [(quant_w, 2, 1), (regroup_w, 3, 0)],
-            8: [(quant_w, 3, 0), (regroup_w, 3, 1)],
-            10: [(quant_w, 3, 1)],
+            1: [(quant_w, 0, 1), (regroup_w, 1, 0)],
+            2: [(regroup_w, 1, 1), (quant_w, 1, 0), (regroup_w, 2, 0)],
+            3: [(quant_w, 1, 1), (regroup_w, 2, 1)],
+            4: [(quant_w, 2, 0)],
+            6: [(quant_w, 2, 1)],
+            7: [(regroup_w, 3, 0)],
+            9: [(quant_w, 3, 0)],
+            10: [(regroup_w, 3, 1)],
+            12: [(quant_w, 3, 1)],
         }
 
-        for j in range(-1, TOTAL + 3):
+        for j in range(-1, TOTAL + 5):
             if ok(j):
                 copy_x(j, 0)
-                copy_x(j, 1)
-            if ok(j - 2):
-                regroup_h(j - 2)
-            if ok(j - 3):
-                add(j - 3, 0)
-                layer2(j - 3, 3)
-                if j - 3 < TOTAL - 1:
-                    relu(j - 3, 0, 1, "G")
-            if ok(j - 1):
-                act(j - 1, 2)
-                act(j - 1, 0)
-                layer1(j - 1, 3)
-                act(j - 1, 1)
-                act(j - 1, 3)
-            if ok(j - 4) and j - 4 < TOTAL - 1:
-                relu(j - 4, 1, 4, "S")
-                store(j - 4, 0, 2)
-                store(j - 4, 2, 4)
             if ok(j + 1):
                 transposes(j + 1, 0)
-                transposes(j + 1, 1)
-            if ok(j - 2):
-                quant_h(j - 2)
-            if ok(j - 3):
-                add(j - 3, 3)
-                add(j - 3, 1)
-                add(j - 3, 2)
-            if j - 3 == TOTAL - 1:
-                relu(j - 3, 0, 1, "S")
-                relu(j - 3, 3, 4, "S")
-                relu(j - 3, 1, 3, "V")
-                store(j - 3, 0, 2)
-                store(j - 3, 2, 4)
+            if ok(j - 1):
+                quant_x(j - 1)
             for step, b, layer in weight_work.get(j, []):
                 step(b, layer)
+            if ok(j - 5):
+                add(j - 5, 0)
+                if j - 5 < TOTAL - 1:
+                    relu(j - 5, 0, 1, "G")
+                layer2(j - 5, 3)
+            if ok(j - 4):
+                quant_h(j - 4)
             if ok(j - 2):
-                layer2(j - 2, 0)
-                layer2(j - 2, 1)
-                layer2(j - 2, 2)
+                act(j - 2, 0)
+            if ok(j - 5):
+                add(j - 5, 2)
+                add(j - 5, 1)
+            if ok(j - 4):
+                layer2(j - 4, 0)
+            if ok(j - 2):
+                layer1(j - 2, 3)
             if ok(j):
-                quant_x(j)
-                layer1(j, 0)
-                layer1(j, 1)
-                layer1(j, 2)
+                copy_x(j, 1)
+            if ok(j + 1):
+                transposes(j + 1, 1)
+            if ok(j - 6) and j - 6 < TOTAL - 1:
+                relu(j - 6, 1, 4, "S")
+                store(j - 6, 0, 2)
+                store(j - 6, 2, 4)
+            if ok(j - 2):
+                act(j - 2, 2)
+                act(j - 2, 1)
+                act(j - 2, 3)
+            if ok(j - 4):
+                layer2(j - 4, 1)
+            if ok(j - 3):
+                regroup_h(j - 3)
+            if ok(j - 5):
+                add(j - 5, 3)
+            if j - 5 == TOTAL - 1:
+                relu(j - 5, 0, 1, "S")
+                relu(j - 5, 1, 3, "S")
+                store(j - 5, 0, 2)
+                relu(j - 5, 3, 4, "V")
+                store(j - 5, 2, 4)
+            if ok(j - 4):
+                layer2(j - 4, 2)
+            if ok(j - 1):
+                layer1(j - 1, 0)
+                layer1(j - 1, 1)
+                layer1(j - 1, 2)
             if 2 <= j < TOTAL - 5:
                 load_x(j + 5)
                 if j == 2:

@@ -19,7 +19,6 @@ PACK = 4
 TILES = 4
 CHUNK = TILES * P
 NCH = NTOK // CHUNK
-APP = NTOK // P
 TOTAL = NB * NCH
 OFF_W = (0, D * D + D)
 OFF_B0 = D * D
@@ -55,8 +54,8 @@ def tile_can_t_kernel(tc, user_emb, item_emb, out):
         def load_x(i):
             b, c = divmod(i, NCH)
             t = const.tile([P, TILES, D], BF16, name="xraw%d" % i)
-            src = user_emb[b].rearrange("(p a) k -> p a k", a=APP)
-            nc.sync.dma_start(out=t[:], in_=src[:, TILES * c : TILES * (c + 1), :])
+            src = user_emb[b, CHUNK * c : CHUNK * (c + 1), :]
+            nc.sync.dma_start(out=t[:], in_=src.rearrange("(p a) k -> p a k", a=TILES))
             xraw[i] = t
 
         b0_sb = const.tile([P, NB, PACK], BF16, name="b0_sb")
@@ -213,8 +212,8 @@ def tile_can_t_kernel(tc, user_emb, item_emb, out):
 
         def store(i, a0, a1):
             b, c = divmod(i, NCH)
-            dst = out[b].rearrange("(m a) e -> m a e", a=APP)
-            nc.sync.dma_start(out=dst[:, TILES * c + a0 : TILES * c + a1, :], in_=st[("osb", i)][:, a0:a1, :])
+            dst = out[b, CHUNK * c : CHUNK * (c + 1), :].rearrange("(m a) e -> m a e", a=TILES)
+            nc.sync.dma_start(out=dst[:, a0:a1, :], in_=st[("osb", i)][:, a0:a1, :])
 
         def ok(i):
             return 0 <= i < TOTAL

@@ -31,13 +31,13 @@ FLOPS = 2 * NB * NTOK * D * D * 2
 def tile_can_t_kernel(tc, user_emb, item_emb, out):
     nc = tc.nc
     with ExitStack() as ctx:
-        ctx.enter_context(tc.manual_schedule())
         const = ctx.enter_context(tc.tile_pool(name="const", bufs=1))
         wstage = ctx.enter_context(tc.tile_pool(name="wstage", bufs=3))
         xq = ctx.enter_context(tc.tile_pool(name="xq", bufs=3))
         hstage = ctx.enter_context(tc.tile_pool(name="hstage", bufs=2))
         hq = ctx.enter_context(tc.tile_pool(name="hq", bufs=2))
         ostage = ctx.enter_context(tc.tile_pool(name="ostage", bufs=4))
+        tstage = ctx.enter_context(tc.tile_pool(name="tstage", bufs=2))
         ps_t = ctx.enter_context(tc.psum_pool(name="ps_t", bufs=2))
         ps_h = ctx.enter_context(tc.psum_pool(name="ps_h", bufs=3))
         ps_o = ctx.enter_context(tc.psum_pool(name="ps_o", bufs=3))
@@ -64,11 +64,16 @@ def tile_can_t_kernel(tc, user_emb, item_emb, out):
         def load_b1(b):
             nc.sync.dma_start(out=b1_bc[:, b, :], in_=item_emb[b, OFF_B1 : OFF_B1 + D].partition_broadcast(P))
 
+        b1rows = const.tile([P, D], BF16, name="b1rows")
+        nc.vector.memset(b1rows[:], 0.0)
+        b1_sb = const.tile([P, PACK, NB], F32, name="b1_sb")
+
         load_w(0, 0)
         load_x(0)
         nc.sync.dma_start(
             out=b0_sb[:], in_=item_emb[:, OFF_B0 : OFF_B0 + D].rearrange("b (p t) -> p b t", t=PACK)
         )
+        nc.sync.dma_start(out=b1rows[0:NB, :], in_=item_emb[:, OFF_B1 : OFF_B1 + D])
         load_w(0, 1)
         load_x(1)
         load_w(1, 0)
@@ -84,6 +89,8 @@ def tile_can_t_kernel(tc, user_emb, item_emb, out):
 
         ident_f = const.tile([P, P], F32, name="ident_f")
         make_identity(nc, ident_f[:])
+        ident_b = const.tile([P, P], BF16, name="ident_b")
+        make_identity(nc, ident_b[:])
 
         wcodes = const.tile([P, 2 * NB, D], U32, name="wcodes", align_bytes=64)
         wscales = const.tile([P, 2 * NB, D], U8, name="wscales", align_bytes=64)
@@ -178,16 +185,23 @@ def tile_can_t_kernel(tc, user_emb, item_emb, out):
             )
             st[("hc", i)] = (hcodes, hscales)
 
+        def turned(i):
+            return i % 3 == 1
+
         def layer2(i, a):
             b = i // NCH
             hcodes, hscales = st[("hc", i)]
             op = ps_o.tile([P, D], F32, name="op", tag="o")
+            part = slice(P * a, P * (a + 1))
+            h = (hcodes, hscales)
+            w = (wcodes[:, 2 * b + 1, :], wscales[:, 2 * b + 1, :])
+            still, moving = (w, h) if turned(i) else (h, w)
             nc.tensor.matmul_mx(
                 out=op[:],
-                lhsT=hcodes[:, P * a : P * (a + 1)].bitcast(FP8X4),
-                lhsT_scale=hscales[:, P * a : P * (a + 1)],
-                rhs=wcodes[:, 2 * b + 1, :].bitcast(FP8X4),
-                rhs_scale=wscales[:, 2 * b + 1, :],
+                lhsT=still[0][:, part].bitcast(FP8X4),
+                lhsT_scale=still[1][:, part],
+                rhs=moving[0][:].bitcast(FP8X4),
+                rhs_scale=moving[1][:],
                 start=True,
                 stop=True,
             )
@@ -200,6 +214,28 @@ def tile_can_t_kernel(tc, user_emb, item_emb, out):
             nc.vector.tensor_tensor(
                 out=st[("osb", i)][:, a, :], in0=st[("op", i, a)][:], in1=b1_bc[:, b, :], op=ALU.add
             )
+
+        def out_act(i, e):
+            if e == 0:
+                st[("oT", i)] = tstage.tile([P, PACK, CHUNK], F32, name="oT", tag="oT")
+            nc.scalar.activation(
+                out=st[("oT", i)][:, e, :],
+                in_=st[("op", i, e)][:],
+                func=ACT.Relu,
+                bias=b1_sb[:, e, i // NCH : i // NCH + 1],
+                scale=1.0,
+            )
+
+        def out_turn(i, a):
+            ot = ps_t.tile([P, PACK, P], F32, name="ot", tag="t")
+            for e in range(PACK):
+                nc.tensor.transpose(ot[:, e, :], st[("oT", i)][:, e, P * a : P * (a + 1)], ident_f[:])
+            st[("ot", i, a)] = ot
+
+        def out_copy(i, a):
+            if a == 0:
+                st[("osb", i)] = ostage.tile([P, TILES, D], F32, name="osb", tag="osb")
+            nc.scalar.copy(out=st[("osb", i)][:, a, :], in_=st[("ot", i, a)][:].rearrange("p e c -> p (e c)"))
 
         def relu(i, a0, a1, engine):
             part = st[("osb", i)][:, a0:a1, :]
@@ -225,67 +261,103 @@ def tile_can_t_kernel(tc, user_emb, item_emb, out):
             3: [(quant_w, 1, 1), (regroup_w, 2, 1)],
             4: [(quant_w, 2, 0)],
             6: [(quant_w, 2, 1)],
-            7: [(regroup_w, 3, 0)],
+            8: [(regroup_w, 3, 0)],
             9: [(quant_w, 3, 0)],
-            10: [(regroup_w, 3, 1)],
+            11: [(regroup_w, 3, 1)],
             12: [(quant_w, 3, 1)],
         }
 
-        for j in range(-1, TOTAL + 5):
+        for j in range(-1, TOTAL + 6):
+            plain = ok(j - 5) and not turned(j - 5)
+            turn = ok(j - 5) and turned(j - 5)
+            leave = ok(j - 6) and turned(j - 6)
             if ok(j):
                 copy_x(j, 0)
-            if ok(j + 1):
+            if leave:
+                out_turn(j - 6, 0)
+            elif ok(j + 1):
                 transposes(j + 1, 0)
             if ok(j - 1):
                 quant_x(j - 1)
+            if ok(j - 6) and not turned(j - 6) and j - 6 < TOTAL - 1:
+                relu(j - 6, 1, 4, "V")
+                store(j - 6, 0, 2)
+                store(j - 6, 2, 4)
             for step, b, layer in weight_work.get(j, []):
                 step(b, layer)
-            if ok(j - 5):
+            if plain:
                 add(j - 5, 0)
                 if j - 5 < TOTAL - 1:
                     relu(j - 5, 0, 1, "G")
+            if turn:
+                out_act(j - 5, 0)
+            if ok(j - 5):
                 layer2(j - 5, 3)
             if ok(j - 4):
                 quant_h(j - 4)
             if ok(j - 2):
                 act(j - 2, 0)
-            if ok(j - 5):
+            if plain:
                 add(j - 5, 2)
                 add(j - 5, 1)
+            if turn:
+                out_act(j - 5, 1)
             if ok(j - 4):
                 layer2(j - 4, 0)
             if ok(j - 2):
                 layer1(j - 2, 3)
             if ok(j):
                 copy_x(j, 1)
-            if ok(j + 1):
+            if leave:
+                out_turn(j - 6, 1)
+            elif ok(j + 1):
                 transposes(j + 1, 1)
-            if ok(j - 6) and j - 6 < TOTAL - 1:
-                relu(j - 6, 1, 4, "S")
-                store(j - 6, 0, 2)
-                store(j - 6, 2, 4)
+            if j == 0:
+                b1T = ps_h.tile([P, PACK, P], BF16, name="b1T", tag="h")
+                for e in range(PACK):
+                    nc.tensor.transpose(b1T[:, e, :], b1rows[:, P * e : P * (e + 1)], ident_b[:])
+                nc.scalar.copy(out=b1_sb[:], in_=b1T[:, :, 0:NB])
+            if leave:
+                out_copy(j - 6, 0)
+                out_turn(j - 6, 2)
             if ok(j - 2):
                 act(j - 2, 2)
-                act(j - 2, 1)
-                act(j - 2, 3)
+            if leave:
+                out_copy(j - 6, 1)
+                out_turn(j - 6, 3)
+            if turn:
+                out_act(j - 5, 2)
             if ok(j - 4):
                 layer2(j - 4, 1)
+            if ok(j - 2):
+                act(j - 2, 1)
+            if leave:
+                out_copy(j - 6, 2)
+            if turn:
+                out_act(j - 5, 3)
             if ok(j - 3):
                 regroup_h(j - 3)
-            if ok(j - 5):
+            if plain:
                 add(j - 5, 3)
             if j - 5 == TOTAL - 1:
-                relu(j - 5, 0, 1, "S")
-                relu(j - 5, 1, 3, "S")
-                store(j - 5, 0, 2)
-                relu(j - 5, 3, 4, "V")
-                store(j - 5, 2, 4)
+                for a, engine in ((0, "S"), (2, "S"), (1, "V"), (3, "V")):
+                    relu(j - 5, a, a + 1, engine)
+                    store(j - 5, a, a + 1)
+            if ok(j - 2):
+                act(j - 2, 3)
+            if leave:
+                out_copy(j - 6, 3)
+                store(j - 6, 0, 2)
+                store(j - 6, 2, 4)
             if ok(j - 4):
                 layer2(j - 4, 2)
             if ok(j - 1):
                 layer1(j - 1, 0)
                 layer1(j - 1, 1)
                 layer1(j - 1, 2)
+            if leave and ok(j + 1):
+                transposes(j + 1, 0)
+                transposes(j + 1, 1)
             if 2 <= j < TOTAL - 5:
                 load_x(j + 5)
                 if j == 2:

@@ -32,11 +32,13 @@ def tile_can_t_kernel(tc, user_emb, item_emb, out):
     nc = tc.nc
     with ExitStack() as ctx:
         const = ctx.enter_context(tc.tile_pool(name="const", bufs=1))
+        wload = ctx.enter_context(tc.tile_pool(name="wload", bufs=6))
+        xload = ctx.enter_context(tc.tile_pool(name="xload", bufs=8))
         wstage = ctx.enter_context(tc.tile_pool(name="wstage", bufs=3))
         xq = ctx.enter_context(tc.tile_pool(name="xq", bufs=3))
-        hstage = ctx.enter_context(tc.tile_pool(name="hstage", bufs=2))
-        hq = ctx.enter_context(tc.tile_pool(name="hq", bufs=2))
-        ostage = ctx.enter_context(tc.tile_pool(name="ostage", bufs=4))
+        hstage = ctx.enter_context(tc.tile_pool(name="hstage", bufs=3))
+        hq = ctx.enter_context(tc.tile_pool(name="hq", bufs=3))
+        ostage = ctx.enter_context(tc.tile_pool(name="ostage", bufs=6))
         tstage = ctx.enter_context(tc.tile_pool(name="tstage", bufs=2))
         ps_t = ctx.enter_context(tc.psum_pool(name="ps_t", bufs=2))
         ps_h = ctx.enter_context(tc.psum_pool(name="ps_h", bufs=3))
@@ -46,14 +48,14 @@ def tile_can_t_kernel(tc, user_emb, item_emb, out):
         xraw = {}
 
         def load_w(b, layer):
-            t = const.tile([P, PACK, D], BF16, name="wraw%d%d" % (b, layer))
+            t = wload.tile([P, PACK, D], BF16, name="wraw", tag="wraw")
             flat = item_emb[b, OFF_W[layer] : OFF_W[layer] + D * D]
             nc.sync.dma_start(out=t[:], in_=flat.rearrange("(p j c) -> p j c", p=P, j=PACK, c=D))
             wraw[(b, layer)] = t
 
         def load_x(i):
             b, c = divmod(i, NCH)
-            t = const.tile([P, TILES, D], BF16, name="xraw%d" % i)
+            t = xload.tile([P, TILES, D], BF16, name="xraw", tag="xraw")
             src = user_emb[b, CHUNK * c : CHUNK * (c + 1), :]
             nc.sync.dma_start(out=t[:], in_=src.rearrange("(p a) k -> p a k", a=TILES))
             xraw[i] = t
@@ -119,6 +121,10 @@ def tile_can_t_kernel(tc, user_emb, item_emb, out):
 
         def transposes(i, half):
             xt = ps_t.tile([P, 2, 2, P], F32, name="xt", tag="t")
+            if i > 0:
+                nc.tensor.matmul(
+                    xt[:].rearrange("p a u r -> p (a u r)"), lhsT=ident_b[:], rhs=b1rows[:], start=True, stop=True
+                )
             for a2 in range(2):
                 words = xraw[i][:, 2 * half + a2, :].bitcast(F32)
                 for u in range(2):

@@ -119,12 +119,13 @@ def tile_can_t_kernel(tc, user_emb, item_emb, out):
 
         st = {}
 
+        def warm(bank):
+            nc.tensor.matmul(bank, lhsT=ident_b[:], rhs=b1rows[:], start=True, stop=True)
+
         def transposes(i, half):
             xt = ps_t.tile([P, 2, 2, P], F32, name="xt", tag="t")
-            if i > 0:
-                nc.tensor.matmul(
-                    xt[:].rearrange("p a u r -> p (a u r)"), lhsT=ident_b[:], rhs=b1rows[:], start=True, stop=True
-                )
+            if i > 2:
+                warm(xt[:].rearrange("p a u r -> p (a u r)"))
             for a2 in range(2):
                 words = xraw[i][:, 2 * half + a2, :].bitcast(F32)
                 for u in range(2):

from contextlib import ExitStack

import concourse.mybir as mybir
from concourse.masks import make_identity

F32 = mybir.dt.float32
BF16 = mybir.dt.bfloat16
U32 = mybir.dt.uint32
U8 = mybir.dt.uint8
FP8X4 = mybir.dt.float8_e4m3fn_x4
ACT = mybir.ActivationFunctionType
ALU = mybir.AluOpType

P = 128
NB = 4
NTOK = 2048
D = 512
PACK = 4
TILES = 4
CHUNK = TILES * P
NCH = NTOK // CHUNK
TOTAL = NB * NCH
OFF_W = (0, D * D + D)
OFF_B0 = D * D
OFF_B1 = 2 * D * D + D
FLT_MAX = 3.4028234663852886e38

FLOPS = 2 * NB * NTOK * D * D * 2


def tile_can_t_kernel(tc, user_emb, item_emb, out):
    nc = tc.nc
    with ExitStack() as ctx:
        const = ctx.enter_context(tc.tile_pool(name="const", bufs=1))
        wload = ctx.enter_context(tc.tile_pool(name="wload", bufs=6))
        xload = ctx.enter_context(tc.tile_pool(name="xload", bufs=8))
        wstage = ctx.enter_context(tc.tile_pool(name="wstage", bufs=3))
        xq = ctx.enter_context(tc.tile_pool(name="xq", bufs=3))
        hstage = ctx.enter_context(tc.tile_pool(name="hstage", bufs=3))
        hq = ctx.enter_context(tc.tile_pool(name="hq", bufs=3))
        ostage = ctx.enter_context(tc.tile_pool(name="ostage", bufs=6))
        tstage = ctx.enter_context(tc.tile_pool(name="tstage", bufs=2))
        ps_t = ctx.enter_context(tc.psum_pool(name="ps_t", bufs=2))
        ps_h = ctx.enter_context(tc.psum_pool(name="ps_h", bufs=3))
        ps_o = ctx.enter_context(tc.psum_pool(name="ps_o", bufs=3))

        wraw = {}
        xraw = {}

        def load_w(b, layer):
            t = wload.tile([P, PACK, D], BF16, name="wraw", tag="wraw")
            flat = item_emb[b, OFF_W[layer] : OFF_W[layer] + D * D]
            nc.sync.dma_start(out=t[:], in_=flat.rearrange("(p j c) -> p j c", p=P, j=PACK, c=D))
            wraw[(b, layer)] = t

        def load_x(i):
            b, c = divmod(i, NCH)
            t = xload.tile([P, TILES, D], BF16, name="xraw", tag="xraw")
            src = user_emb[b, CHUNK * c : CHUNK * (c + 1), :]
            nc.sync.dma_start(out=t[:], in_=src.rearrange("(p a) k -> p a k", a=TILES))
            xraw[i] = t

        b0_sb = const.tile([P, NB, PACK], BF16, name="b0_sb")
        b1_bc = const.tile([P, NB, D], BF16, name="b1_bc")

        def load_b1(b):
            nc.sync.dma_start(out=b1_bc[:, b, :], in_=item_emb[b, OFF_B1 : OFF_B1 + D].partition_broadcast(P))

        b1rows = const.tile([P, D], BF16, name="b1rows")
        nc.vector.memset(b1rows[:], 0.0)
        b1_sb = const.tile([P, PACK, NB], F32, name="b1_sb")

        load_w(0, 0)
        load_x(0)
        nc.sync.dma_start(
            out=b0_sb[:], in_=item_emb[:, OFF_B0 : OFF_B0 + D].rearrange("b (p t) -> p b t", t=PACK)
        )
        nc.sync.dma_start(out=b1rows[0:NB, :], in_=item_emb[:, OFF_B1 : OFF_B1 + D])
        load_w(0, 1)
        load_x(1)
        load_w(1, 0)
        load_w(1, 1)
        load_x(2)
        load_b1(0)
        load_w(2, 0)
        load_x(3)
        load_w(2, 1)
        load_x(4)
        load_x(5)
        load_x(6)

        ident_f = const.tile([P, P], F32, name="ident_f")
        make_identity(nc, ident_f[:])
        ident_b = const.tile([P, P], BF16, name="ident_b")
        make_identity(nc, ident_b[:])

        wcodes = const.tile([P, 2 * NB, D], U32, name="wcodes", align_bytes=64)
        wscales = const.tile([P, 2 * NB, D], U8, name="wscales", align_bytes=64)
        wgrp = {}

        def regroup_w(b, layer):
            grp = wstage.tile([P, D, PACK], BF16, name="wgrp", tag="wgrp", align_bytes=64)
            if layer == 0:
                dst = grp[:].rearrange("p (t m) j -> p m j t", t=PACK)
                src = wraw[(b, layer)][:].rearrange("p j (m t) -> p m j t", t=PACK)
            else:
                dst = grp[:].rearrange("p (c i) j -> p c j i", i=4)
                src = wraw[(b, layer)][:].rearrange("p j (c i) -> p c j i", i=4)
            nc.vector.tensor_copy(out=dst, in_=src)
            wgrp[(b, layer)] = grp

        def quant_w(b, layer):
            j = 2 * b + layer
            nc.vector.quantize_mx(
                out=wcodes[:, j, :].bitcast(FP8X4),
                scales=wscales[:, j, :],
                in_=wgrp[(b, layer)][:].rearrange("p c t -> p (c t)"),
            )

        st = {}

        def warm(bank):
            nc.tensor.matmul(bank, lhsT=ident_b[:], rhs=b1rows[:], start=True, stop=True)

        def transposes(i, half):
            xt = ps_t.tile([P, 2, 2, P], F32, name="xt", tag="t")
            if i > 2:
                warm(xt[:].rearrange("p a u r -> p (a u r)"))
            for a2 in range(2):
                words = xraw[i][:, 2 * half + a2, :].bitcast(F32)
                for u in range(2):
                    nc.tensor.transpose(xt[:, a2, u, :], words[:, u : 2 * P : 2], ident_f[:])
            st[("xt", i, half)] = xt

        def copy_x(i, half):
            if half == 0:
                st[("xgrp", i)] = xq.tile([P, CHUNK * PACK], BF16, name="xgrp", tag="xgrp", align_bytes=64)
            xw = st[("xgrp", i)][:].bitcast(F32).rearrange("p (a r u) -> p a r u", a=TILES, r=P, u=2)
            nc.scalar.copy(
                out=xw[:, 2 * half : 2 * half + 2, :, :],
                in_=st[("xt", i, half)][:].rearrange("p a u r -> p a r u"),
            )

        def quant_x(i):
            xcodes = xq.tile([P, CHUNK], U32, name="xcodes", tag="xcodes", align_bytes=64)
            xscales = xq.tile([P, CHUNK], U8, name="xscales", tag="xscales", align_bytes=64)
            nc.vector.quantize_mx(out=xcodes[:].bitcast(FP8X4), scales=xscales[:], in_=st[("xgrp", i)][:])
            st[("xc", i)] = (xcodes, xscales)

        def layer1(i, t):
            b = i // NCH
            xcodes, xscales = st[("xc", i)]
            hp = ps_h.tile([P, CHUNK], F32, name="hp", tag="h")
            nc.tensor.matmul_mx(
                out=hp[:],
                lhsT=wcodes[:, 2 * b, P * t : P * (t + 1)].bitcast(FP8X4),
                lhsT_scale=wscales[:, 2 * b, P * t : P * (t + 1)],
                rhs=xcodes[:].bitcast(FP8X4),
                rhs_scale=xscales[:],
                start=True,
                stop=True,
            )
            st[("hp", i, t)] = hp

        def act(i, t):
            b = i // NCH
            if ("hT", i) not in st:
                st[("hT", i)] = hstage.tile([P, PACK, CHUNK], BF16, name="hT", tag="hT")
            nc.scalar.activation(
                out=st[("hT", i)][:, t, :],
                in_=st[("hp", i, t)][:],
                func=ACT.Relu,
                bias=b0_sb[:, b, t : t + 1],
                scale=1.0,
            )

        def regroup_h(i):
            hgrp = hq.tile([P, CHUNK, PACK], BF16, name="hgrp", tag="hgrp", align_bytes=64)
            nc.vector.tensor_copy(
                out=hgrp[:].rearrange("p (c i) t -> p c t i", i=4),
                in_=st[("hT", i)][:].rearrange("p t (c i) -> p c t i", i=4),
            )
            st[("hgrp", i)] = hgrp

        def quant_h(i):
            hcodes = hq.tile([P, CHUNK], U32, name="hcodes", tag="hcodes", align_bytes=64)
            hscales = hq.tile([P, CHUNK], U8, name="hscales", tag="hscales", align_bytes=64)
            nc.vector.quantize_mx(
                out=hcodes[:].bitcast(FP8X4),
                scales=hscales[:],
                in_=st[("hgrp", i)][:].rearrange("p c t -> p (c t)"),
            )
            st[("hc", i)] = (hcodes, hscales)

        def turned(i):
            return i % 3 == 1

        def layer2(i, a):
            b = i // NCH
            hcodes, hscales = st[("hc", i)]
            op = ps_o.tile([P, D], F32, name="op", tag="o")
            part = slice(P * a, P * (a + 1))
            h = (hcodes, hscales)
            w = (wcodes[:, 2 * b + 1, :], wscales[:, 2 * b + 1, :])
            still, moving = (w, h) if turned(i) else (h, w)
            nc.tensor.matmul_mx(
                out=op[:],
                lhsT=still[0][:, part].bitcast(FP8X4),
                lhsT_scale=still[1][:, part],
                rhs=moving[0][:].bitcast(FP8X4),
                rhs_scale=moving[1][:],
                start=True,
                stop=True,
            )
            st[("op", i, a)] = op

        def add(i, a):
            b = i // NCH
            if a == 0:
                st[("osb", i)] = ostage.tile([P, TILES, D], F32, name="osb", tag="osb")
            nc.vector.tensor_tensor(
                out=st[("osb", i)][:, a, :], in0=st[("op", i, a)][:], in1=b1_bc[:, b, :], op=ALU.add
            )

        def out_act(i, e):
            if e == 0:
                st[("oT", i)] = tstage.tile([P, PACK, CHUNK], F32, name="oT", tag="oT")
            nc.scalar.activation(
                out=st[("oT", i)][:, e, :],
                in_=st[("op", i, e)][:],
                func=ACT.Relu,
                bias=b1_sb[:, e, i // NCH : i // NCH + 1],
                scale=1.0,
            )

        def out_turn(i, a):
            ot = ps_t.tile([P, PACK, P], F32, name="ot", tag="t")
            for e in range(PACK):
                nc.tensor.transpose(ot[:, e, :], st[("oT", i)][:, e, P * a : P * (a + 1)], ident_f[:])
            st[("ot", i, a)] = ot

        def out_copy(i, a):
            if a == 0:
                st[("osb", i)] = ostage.tile([P, TILES, D], F32, name="osb", tag="osb")
            nc.scalar.copy(out=st[("osb", i)][:, a, :], in_=st[("ot", i, a)][:].rearrange("p e c -> p (e c)"))

        def relu(i, a0, a1, engine):
            part = st[("osb", i)][:, a0:a1, :]
            if engine == "S":
                nc.scalar.activation(out=part, in_=part, func=ACT.Relu)
            elif engine == "V":
                nc.vector.tensor_scalar_max(out=part, in0=part, scalar1=0.0)
            else:
                nc.gpsimd.tensor_scalar(out=part, in0=part, scalar1=FLT_MAX, scalar2=0.0, op0=ALU.min, op1=ALU.max)

        def store(i, a0, a1):
            b, c = divmod(i, NCH)
            dst = out[b, CHUNK * c : CHUNK * (c + 1), :].rearrange("(m a) e -> m a e", a=TILES)
            nc.sync.dma_start(out=dst[:, a0:a1, :], in_=st[("osb", i)][:, a0:a1, :])

        def ok(i):
            return 0 <= i < TOTAL

        weight_work = {
            -1: [(regroup_w, 0, 0), (quant_w, 0, 0), (regroup_w, 0, 1)],
            1: [(quant_w, 0, 1), (regroup_w, 1, 0)],
            2: [(regroup_w, 1, 1), (quant_w, 1, 0), (regroup_w, 2, 0)],
            3: [(quant_w, 1, 1), (regroup_w, 2, 1)],
            4: [(quant_w, 2, 0)],
            6: [(quant_w, 2, 1)],
            8: [(regroup_w, 3, 0)],
            9: [(quant_w, 3, 0)],
            11: [(regroup_w, 3, 1)],
            12: [(quant_w, 3, 1)],
        }

        for j in range(-1, TOTAL + 6):
            plain = ok(j - 5) and not turned(j - 5)
            turn = ok(j - 5) and turned(j - 5)
            leave = ok(j - 6) and turned(j - 6)
            if ok(j):
                copy_x(j, 0)
            if leave:
                out_turn(j - 6, 0)
            elif ok(j + 1):
                transposes(j + 1, 0)
            if ok(j - 1):
                quant_x(j - 1)
            if ok(j - 6) and not turned(j - 6) and j - 6 < TOTAL - 1:
                relu(j - 6, 1, 4, "V")
                store(j - 6, 0, 2)
                store(j - 6, 2, 4)
            for step, b, layer in weight_work.get(j, []):
                step(b, layer)
            if plain:
                add(j - 5, 0)
                if j - 5 < TOTAL - 1:
                    relu(j - 5, 0, 1, "G")
            if turn:
                out_act(j - 5, 0)
            if ok(j - 5):
                layer2(j - 5, 3)
            if ok(j - 4):
                quant_h(j - 4)
            if ok(j - 2):
                act(j - 2, 0)
            if plain:
                add(j - 5, 2)
                add(j - 5, 1)
            if turn:
                out_act(j - 5, 1)
            if ok(j - 4):
                layer2(j - 4, 0)
            if ok(j - 2):
                layer1(j - 2, 3)
            if ok(j):
                copy_x(j, 1)
            if leave:
                out_turn(j - 6, 1)
            elif ok(j + 1):
                transposes(j + 1, 1)
            if j == 0:
                b1T = ps_h.tile([P, PACK, P], BF16, name="b1T", tag="h")
                for e in range(PACK):
                    nc.tensor.transpose(b1T[:, e, :], b1rows[:, P * e : P * (e + 1)], ident_b[:])
                nc.scalar.copy(out=b1_sb[:], in_=b1T[:, :, 0:NB])
            if leave:
                out_copy(j - 6, 0)
                out_turn(j - 6, 2)
            if ok(j - 2):
                act(j - 2, 2)
            if leave:
                out_copy(j - 6, 1)
                out_turn(j - 6, 3)
            if turn:
                out_act(j - 5, 2)
            if ok(j - 4):
                layer2(j - 4, 1)
            if ok(j - 2):
                act(j - 2, 1)
            if leave:
                out_copy(j - 6, 2)
            if turn:
                out_act(j - 5, 3)
            if ok(j - 3):
                regroup_h(j - 3)
            if plain:
                add(j - 5, 3)
            if j - 5 == TOTAL - 1:
                for a, engine in ((0, "S"), (2, "S"), (1, "V"), (3, "V")):
                    relu(j - 5, a, a + 1, engine)
                    store(j - 5, a, a + 1)
            if ok(j - 2):
                act(j - 2, 3)
            if leave:
                out_copy(j - 6, 3)
                store(j - 6, 0, 2)
                store(j - 6, 2, 4)
            if ok(j - 4):
                layer2(j - 4, 2)
            if ok(j - 1):
                layer1(j - 1, 0)
                layer1(j - 1, 1)
                layer1(j - 1, 2)
            if leave and ok(j + 1):
                transposes(j + 1, 0)
                transposes(j + 1, 1)
            if 2 <= j < TOTAL - 5:
                load_x(j + 5)
                if j == 2:
                    load_b1(1)
                if j == 3:
                    load_w(3, 0)
                if j == 4:
                    load_b1(2)
                if j == 5:
                    load_w(3, 1)
                if j == 6:
                    load_b1(3)
